import numpy as np
import ml_dtypes


def mxq(x, axis, fmt="e4m3"):
    dtype, down = {"e4m3": (ml_dtypes.float8_e4m3fn, 7), "e5m2": (ml_dtypes.float8_e5m2, 14)}[fmt]
    v = np.moveaxis(np.asarray(x, np.float32).astype(ml_dtypes.bfloat16).astype(np.float64), axis, -1)
    blocks = v.reshape(v.shape[:-1] + (-1, 32))
    amax = np.abs(blocks).max(-1, keepdims=True)
    byte = np.maximum(np.where(amax > 0, np.frexp(amax)[1] - 1 + 127, 0) - down, 1)
    scale = np.exp2(byte - 127.0)
    codes = (blocks / scale).astype(np.float32).astype(dtype).astype(np.float64)
    return np.moveaxis((codes * scale).reshape(v.shape), -1, axis)


WIDE = False


def mx_kscale(k):
    if not WIDE:
        return np.ones(k)
    levels = np.array([10, -10, 5, -5, 0])
    a = np.random.permutation(np.resize(levels, k // 512 * 4)).reshape(k // 512, 4)
    idx = np.arange(k)
    return np.exp2(a[idx // 512, idx % 128 // 32])


BF16 = ml_dtypes.bfloat16


def bf(x):
    return np.asarray(x, np.float32).astype(BF16)


def f64(x):
    return np.asarray(x).astype(np.float64)


B, S, D, E = 4, 4096, 512, 128
INV_SQRT2 = 0.7071067811865476


def dwt_haar(x):
    e = x[..., 0::2]
    o = x[..., 1::2]
    return (e + o) * INV_SQRT2, (o - e) * INV_SQRT2


def idwt_haar(L, H):
    a = (L - H) * INV_SQRT2
    b = (L + H) * INV_SQRT2
    return np.stack([a, b], axis=-1).reshape(*L.shape[:-1], -1)


def softmax(v):
    p = np.exp(v - v.max(-1, keepdims=True))
    return p / p.sum(-1, keepdims=True)


def setup_inputs():
    s = mx_kscale(D)
    return {"x": bf(np.random.standard_normal((B, S, D)) * s),
            "W_q": bf(np.random.standard_normal((E, D)) * 1.5 / np.sqrt(D) / s),
            "b_q": bf(np.random.standard_normal(E) * 0.5),
            "W_k": bf(np.random.standard_normal((E, D)) * 1.5 / np.sqrt(D) / s),
            "b_k": bf(np.random.standard_normal(E) * 0.5),
            "W_v": bf(np.random.standard_normal((E, D)) * 2.0 / np.sqrt(D) / s),
            "b_v": bf(np.random.standard_normal(E) * 0.5)}


def reference(x, W_q, b_q, W_k, b_k, W_v, b_v):
    nb, ns = x.shape[0], x.shape[1]
    xq = mxq(f64(x), 2, "e4m3")
    q = (xq @ mxq(f64(W_q), 1, "e4m3").T) + f64(b_q)
    k = (xq @ mxq(f64(W_k), 1, "e4m3").T) + f64(b_k)
    v = (xq @ mxq(f64(W_v), 1, "e4m3").T) + f64(b_v)
    q_L, q_H = dwt_haar(q)
    k_L, k_H = dwt_haar(k)
    v_L, v_H = dwt_haar(v)
    L = softmax(q_L + k_L)
    H = softmax(q_H + k_H)
    L_out = softmax(L + v_L)
    H_out = softmax(H + v_H)
    out = idwt_haar(L_out, H_out)
    return out.reshape(nb, ns, -1)

@@ -1,0 +1,347 @@
+from contextlib import ExitStack
+
+import concourse.mybir as mybir
+from concourse.masks import make_identity
+
+F32 = mybir.dt.float32
+BF16 = mybir.dt.bfloat16
+U32 = mybir.dt.uint32
+U8 = mybir.dt.uint8
+FP8X4 = mybir.dt.float8_e4m3fn_x4
+ALU = mybir.AluOpType
+ACTF = mybir.ActivationFunctionType
+AX = mybir.AxisListType
+
+P = 128
+D = 512
+E = 128
+HALF = 64
+TOKENS = 4 * 4096
+SLOTS = TOKENS // P
+GS = 4
+NG = SLOTS // GS
+CH = 8
+NCH = SLOTS // CH
+C = 0.7071067811865476
+SA = 2
+LEAD = 4
+TAIL = 3
+
+FLOPS = 2 * TOKENS * D * 3 * E
+
+
+def tile_waveletmultiheadattention_t_kernel(tc, x, W_q, b_q, W_k, b_k, W_v, b_v, out):
+    nc = tc.nc
+    xv = x.flatten_outer_dims().rearrange("(p t) k -> p t k", p=P)
+    ov = out.flatten_outer_dims().rearrange("(p t) f -> p t f", p=P)
+
+    with ExitStack() as ctx:
+        const = ctx.enter_context(tc.tile_pool(name="const", bufs=1))
+        xpool = ctx.enter_context(tc.tile_pool(name="xpool", bufs=4))
+        gpool = ctx.enter_context(tc.tile_pool(name="gpool", bufs=3))
+        qpool = ctx.enter_context(tc.tile_pool(name="qpool", bufs=3))
+        work = ctx.enter_context(tc.tile_pool(name="work", bufs=4))
+        small = ctx.enter_context(tc.tile_pool(name="small", bufs=6))
+        psx = ctx.enter_context(tc.psum_pool(name="psx", bufs=4))
+        pst = ctx.enter_context(tc.psum_pool(name="pst", bufs=2))
+        ctx.enter_context(tc.manual_schedule())
+
+        live = {}
+
+        def load(c):
+            x_sb = xpool.tile([P, CH * D], BF16, tag="x")
+            nc.sync.dma_start(
+                out=x_sb[:], in_=xv[:, c * CH : (c + 1) * CH, :].rearrange("p t k -> p (t k)")
+            )
+            live[("x", c)] = x_sb
+
+        w_sb = const.tile([P, 3 * D], BF16)
+        for i, w in enumerate((W_q, W_k, W_v)):
+            nc.scalar.dma_start(out=w_sb[:, i * D : (i + 1) * D], in_=w)
+        x_first = xpool.tile([P, CH * D], BF16, tag="x")
+        for hf in range(2):
+            nc.sync.dma_start(
+                out=x_first[:, hf * GS * D : (hf + 1) * GS * D],
+                in_=xv[:, hf * GS : (hf + 1) * GS, :].rearrange("p t k -> p (t k)"),
+            )
+        live[("x", 0)] = x_first
+        load(1)
+        bb = const.tile([P, 3, E], BF16)
+        for i, b in enumerate((b_q, b_k, b_v)):
+            nc.scalar.dma_start(out=bb[:, i, :], in_=b.partition_broadcast(P))
+
+        ident = const.tile([P, P], F32)
+        make_identity(nc, ident[:])
+
+        warm_in = const.tile([P, 1], F32)
+        warm_out = const.tile([P, 1], F32)
+        nc.vector.memset(warm_in[:], 0.0)
+        nc.scalar.activation(out=warm_out[:], in_=warm_in[:], func=ACTF.Exp)
+
+        ww = w_sb[:].bitcast(F32)
+        wg = const.tile([P, 6 * E * 4], BF16, align_bytes=64)
+        wgf = wg[:].bitcast(F32).rearrange("p (w q h j u) -> p w q h j u", w=3, q=2, h=2, u=2)
+        wgw = wg[:].bitcast(F32).rearrange("p (w q h c) -> p w q h c", w=3, q=2, h=2)
+        wgb = wg[:].rearrange("p (w q h c) -> p w q h c", w=3, q=2, h=2)
+        for i in range(3):
+            wt = psx.tile([P, 512], F32, tag="xt")
+            for u in range(2):
+                nc.tensor.transpose(
+                    wt[:, u * P : (u + 1) * P], ww[:, i * 256 + u * P : i * 256 + (u + 1) * P], ident[:]
+                )
+            nc.vector.tensor_copy(
+                out=wgf[:, i, :, 0, :, :],
+                in_=wt[:, 0:256].rearrange("p (u j q) -> p q j u", u=2, q=2),
+            )
+        nc.vector.tensor_copy(out=wgw[:, :, 1, 1, :], in_=wgw[:, :, 1, 0, :])
+        nc.vector.tensor_scalar(
+            out=wgb[:, :, 0, 1, :], in0=wgb[:, :, 0, 0, :], scalar1=-1.0, scalar2=None, op0=ALU.mult
+        )
+        wcodes = const.tile([P, 6 * E], U32, align_bytes=64)
+        wscales = const.tile([P, 6 * E], U8, align_bytes=64)
+        nc.vector.quantize_mx(
+            out=wcodes[:, 0:512].bitcast(FP8X4), scales=wscales[:, 0:512], in_=wg[:, 0:2048]
+        )
+        nc.vector.quantize_mx(
+            out=wcodes[:, 512:768].bitcast(FP8X4), scales=wscales[:, 512:768], in_=wg[:, 2048:3072]
+        )
+
+        bh = const.tile([P, 2, E], F32)
+
+        def prepare_biases():
+            bs = const.tile([P, 2, E], F32)
+            nc.vector.tensor_tensor(out=bs[:, 0, :], in0=bb[:, 0, :], in1=bb[:, 1, :], op=ALU.add)
+            nc.vector.tensor_copy(out=bs[:, 1, :], in_=bb[:, 2, :])
+            bsv = bs[:].rearrange("p a (j q) -> p a j q", q=2)
+            bh0 = const.tile([P, 2, 2, HALF], F32)
+            nc.vector.tensor_tensor(
+                out=bh0[:, :, 0, :], in0=bsv[:, :, :, 0], in1=bsv[:, :, :, 1], op=ALU.add
+            )
+            nc.vector.tensor_tensor(
+                out=bh0[:, :, 1, :], in0=bsv[:, :, :, 1], in1=bsv[:, :, :, 0], op=ALU.subtract
+            )
+            nc.vector.tensor_scalar(
+                out=bh[:].rearrange("p a f -> p (a f)"),
+                in0=bh0[:].rearrange("p a h j -> p (a h j)"),
+                scalar1=C,
+                scalar2=None,
+                op0=ALU.mult,
+            )
+
+        def halves(lo, hi):
+            return [(h, slice(h * HALF, (h + 1) * HALF)) for h in range(lo, hi)]
+
+        def transposes(g):
+            xw = live[("x", g // 2)][:].bitcast(F32)
+            base = (g % 2) * 1024
+            for b in range(2):
+                xt = psx.tile([P, 512], F32, tag="xt")
+                for i in range(4):
+                    o = base + b * 512 + i * P
+                    nc.tensor.transpose(xt[:, i * P : (i + 1) * P], xw[:, o : o + P], ident[:])
+                live[("xt", g, b)] = xt
+
+        def evacuate(g):
+            grouped = gpool.tile([P, GS * P * 4], BF16, tag="grouped", align_bytes=64)
+            gf = grouped[:].bitcast(F32)
+            for b in range(2):
+                nc.scalar.copy(
+                    out=gf[:, b * 512 : (b + 1) * 512].rearrange("p (s r u) -> p s r u", s=2, u=2),
+                    in_=live[("xt", g, b)][:].rearrange("p (s u r) -> p s r u", s=2, u=2),
+                )
+            live[("grouped", g)] = grouped
+
+        def quantise(g):
+            codes = qpool.tile([P, GS * P], U32, tag="codes", align_bytes=64)
+            scales = qpool.tile([P, GS * P], U8, tag="scales", align_bytes=64)
+            nc.vector.quantize_mx(
+                out=codes[:].bitcast(FP8X4), scales=scales[:], in_=live[("grouped", g)][:]
+            )
+            live[("codes", g)] = codes
+            live[("scales", g)] = scales
+
+        def passes(g):
+            codes = live[("codes", g)]
+            scales = live[("scales", g)]
+            t_ps = pst.tile([P, GS * E], F32, tag="T")
+            v_ps = pst.tile([P, GS * E], F32, tag="V")
+            for dst, blks in ((t_ps, (0, 1, 2, 3)), (v_ps, (4, 5))):
+                for s in range(GS):
+                    cs = slice(s * P, (s + 1) * P)
+                    for n, blk in enumerate(blks):
+                        nc.tensor.matmul_mx(
+                            out=dst[:, cs],
+                            lhsT=codes[:, cs].bitcast(FP8X4),
+                            lhsT_scale=scales[:, cs],
+                            rhs=wcodes[:, blk * E : (blk + 1) * E].bitcast(FP8X4),
+                            rhs_scale=wscales[:, blk * E : (blk + 1) * E],
+                            start=(n == 0),
+                            stop=(n == len(blks) - 1),
+                        )
+            live[("ps", g, 0)] = t_ps
+            live[("ps", g, 1)] = v_ps
+
+        def bias_add(g, a):
+            dst = work.tile([P, GS * E], F32, tag="uv%d" % a, name="uv%d" % a)
+            nc.vector.scalar_tensor_tensor(
+                out=dst[:].rearrange("p (s f) -> p s f", f=E),
+                in0=live[("ps", g, a)][:].rearrange("p (s f) -> p s f", f=E),
+                scalar=C,
+                in1=bh[:, a, :].unsqueeze(1).to_broadcast([P, GS, E]),
+                op0=ALU.mult,
+                op1=ALU.add,
+            )
+            live[("uv", g, a)] = dst
+
+        def neg_max(g, a):
+            nm = small.tile([P, 2 * GS], F32, tag="nm%d" % a, name="nm%d" % a)
+            nc.vector.tensor_reduce(
+                out=nm[:], in_=live[("uv", g, a)][:].rearrange("p (g j) -> p g j", j=HALF), axis=AX.X,
+                op=ALU.max, negate=True,
+            )
+            live[("nm", g, a)] = nm
+
+        def exp1(g, lo, hi):
+            if lo == 0:
+                e1_new = work.tile([P, GS * E], F32, tag="e1")
+                s1_new = small.tile([P, 2 * GS], F32, tag="s1")
+                live[("e1", g)] = e1_new
+                live[("s1", g)] = s1_new
+            e1 = live[("e1", g)]
+            s1 = live[("s1", g)]
+            u_sb = live[("uv", g, 0)]
+            nm1 = live[("nm", g, 0)]
+            for h, hs in halves(lo, hi):
+                nc.scalar.activation(
+                    out=e1[:, hs], in_=u_sb[:, hs], func=ACTF.Exp, bias=nm1[:, h : h + 1], scale=1.0,
+                    accum_out=s1[:, h : h + 1],
+                )
+
+        def recip1(g):
+            r1 = small.tile([P, 2 * GS], F32, tag="r1")
+            nc.vector.reciprocal(out=r1[:], in_=live[("s1", g)][:])
+            live[("r1", g)] = r1
+
+        def add_v(g):
+            w_t = work.tile([P, GS * E], F32, tag="w")
+            e1 = live[("e1", g)]
+            r1 = live[("r1", g)]
+            vb_sb = live[("uv", g, 1)]
+            for h, hs in halves(0, 2 * GS):
+                nc.vector.scalar_tensor_tensor(
+                    out=w_t[:, hs], in0=e1[:, hs], scalar=r1[:, h : h + 1], in1=vb_sb[:, hs],
+                    op0=ALU.mult, op1=ALU.add,
+                )
+            live[("w", g)] = w_t
+
+        def exp2(g):
+            e2 = work.tile([P, GS * E], F32, tag="e2")
+            s2 = small.tile([P, 2 * GS], F32, tag="s2")
+            w_t = live[("w", g)]
+            nm2 = live[("nm", g, 1)]
+            for h, hs in halves(0, 2 * GS):
+                nc.scalar.activation(
+                    out=e2[:, hs], in_=w_t[:, hs], func=ACTF.Exp, bias=nm2[:, h : h + 1], scale=1.0,
+                    accum_out=s2[:, h : h + 1],
+                )
+            live[("e2", g)] = e2
+            live[("s2", g)] = s2
+
+        def scale_sums(g):
+            s2c = small.tile([P, 2 * GS], F32, tag="s2c")
+            nc.scalar.mul(out=s2c[:], in_=live[("s2", g)][:], mul=1.0 / C)
+            live[("s2c", g)] = s2c
+
+        def scalar_slots(g):
+            return GS if g >= NG - TAIL else SA
+
+        def recip2(g, part):
+            sa = scalar_slots(g)
+            lo, hi = ((0, 2 * sa), (2 * sa, 2 * GS))[part]
+            if lo == hi:
+                return
+            r2c = small.tile([P, hi - lo], F32, tag="r2c%d" % part, name="r2c%d" % part)
+            nc.vector.reciprocal(out=r2c[:], in_=live[("s2c", g)][:, lo:hi])
+            live[("r2c", g, part)] = r2c
+
+        def finish_scalar(g):
+            sa = scalar_slots(g)
+            e2 = live[("e2", g)]
+            r2c = live[("r2c", g, 0)]
+            na = work.tile([P, sa * E], F32, tag="na")
+            for h, hs in halves(0, 2 * sa):
+                nc.scalar.activation(out=na[:, hs], in_=e2[:, hs], func=ACTF.Copy, scale=r2c[:, h : h + 1])
+            live[("na", g)] = na
+
+        def finish_butterfly(g):
+            sa = scalar_slots(g)
+            e2 = live[("e2", g)]
+            na = live[("na", g)]
+            o_t = work.tile([P, GS * E], F32, tag="o")
+            o4 = o_t[:].rearrange("p (s j e) -> p s j e", j=HALF, e=2)
+            if sa < GS:
+                npl = work.tile([P, (GS - sa) * E], F32, tag="npl")
+                nc.gpsimd.tensor_tensor(
+                    out=npl[:].rearrange("p (g j) -> p g j", j=HALF),
+                    in0=e2[:, sa * E :].rearrange("p (g j) -> p g j", j=HALF),
+                    in1=live[("r2c", g, 1)][:].unsqueeze(2).to_broadcast([P, 2 * (GS - sa), HALF]),
+                    op=ALU.mult,
+                )
+                pieces = ((nc.gpsimd, na[:], 0, sa), (nc.gpsimd, npl[:], sa, GS))
+            else:
+                pieces = (
+                    (nc.vector, na[:, : 2 * E], 0, 2),
+                    (nc.gpsimd, na[:, 2 * E :], 2, GS),
+                )
+            for eng, src, lo, hi in pieces:
+                nv = src.rearrange("p (s h j) -> p s h j", h=2, j=HALF)
+                eng.tensor_tensor(
+                    out=o4[:, lo:hi, :, 0], in0=nv[:, :, 0, :], in1=nv[:, :, 1, :], op=ALU.subtract
+                )
+                eng.tensor_tensor(
+                    out=o4[:, lo:hi, :, 1], in0=nv[:, :, 0, :], in1=nv[:, :, 1, :], op=ALU.add
+                )
+            nc.sync.dma_start(
+                out=ov[:, g * GS : (g + 1) * GS, :].rearrange("p t f -> p (t f)"), in_=o_t[:]
+            )
+
+        def ok(g):
+            return 0 <= g < NG
+
+        for i in range(-3, NG + 4):
+            nxt = i + 3 + LEAD
+            if nxt % 2 == 0 and 2 <= nxt // 2 < NCH:
+                load(nxt // 2)
+            if ok(i + 1):
+                passes(i + 1)
+            if ok(i + 3):
+                transposes(i + 3)
+            if ok(i - 4):
+                recip2(i - 4, 1)
+                finish_scalar(i - 4)
+                finish_butterfly(i - 4)
+            if ok(i + 2):
+                evacuate(i + 2)
+            if ok(i):
+                bias_add(i, 0)
+                bias_add(i, 1)
+                neg_max(i, 0)
+                neg_max(i, 1)
+            if ok(i - 1):
+                recip1(i - 1)
+            if ok(i - 3):
+                recip2(i - 3, 0)
+            if ok(i + 2):
+                quantise(i + 2)
+            if i == -1:
+                prepare_biases()
+            if ok(i - 2):
+                exp2(i - 2)
+            if ok(i):
+                exp1(i, 0, 2)
+            if ok(i - 2):
+                scale_sums(i - 2)
+            if ok(i):
+                exp1(i, 2, 2 * GS)
+            if ok(i - 1):
+                add_v(i - 1)

@@ -23,7 +23,7 @@ NG = SLOTS // GS
 CH = 8
 NCH = SLOTS // CH
 C = 0.7071067811865476
-SA = 2
+NSC = 7
 LEAD = 4
 TAIL = 3
 
@@ -57,7 +57,7 @@ def tile_waveletmultiheadattention_t_kernel(tc, x, W_q, b_q, W_k, b_k, W_v, b_v,
 
         w_sb = const.tile([P, 3 * D], BF16)
         for i, w in enumerate((W_q, W_k, W_v)):
-            nc.scalar.dma_start(out=w_sb[:, i * D : (i + 1) * D], in_=w)
+            nc.sync.dma_start(out=w_sb[:, i * D : (i + 1) * D], in_=w)
         x_first = xpool.tile([P, CH * D], BF16, tag="x")
         for hf in range(2):
             nc.sync.dma_start(
@@ -252,46 +252,38 @@ def tile_waveletmultiheadattention_t_kernel(tc, x, W_q, b_q, W_k, b_k, W_v, b_v,
             nc.scalar.mul(out=s2c[:], in_=live[("s2", g)][:], mul=1.0 / C)
             live[("s2c", g)] = s2c
 
-        def scalar_slots(g):
-            return GS if g >= NG - TAIL else SA
+        def recip2(g):
+            r2c = small.tile([P, 2 * GS], F32, tag="r2c")
+            nc.vector.reciprocal(out=r2c[:], in_=live[("s2c", g)][:])
+            live[("r2c", g)] = r2c
 
-        def recip2(g, part):
-            sa = scalar_slots(g)
-            lo, hi = ((0, 2 * sa), (2 * sa, 2 * GS))[part]
-            if lo == hi:
-                return
-            r2c = small.tile([P, hi - lo], F32, tag="r2c%d" % part, name="r2c%d" % part)
-            nc.vector.reciprocal(out=r2c[:], in_=live[("s2c", g)][:, lo:hi])
-            live[("r2c", g, part)] = r2c
-
-        def finish_scalar(g):
-            sa = scalar_slots(g)
+        def finish_scalar(g, lo, hi):
+            if lo == 0:
+                na_new = work.tile([P, GS * E], F32, tag="na")
+                live[("na", g)] = na_new
             e2 = live[("e2", g)]
-            r2c = live[("r2c", g, 0)]
-            na = work.tile([P, sa * E], F32, tag="na")
-            for h, hs in halves(0, 2 * sa):
+            r2c = live[("r2c", g)]
+            na = live[("na", g)]
+            for h, hs in halves(lo, hi):
                 nc.scalar.activation(out=na[:, hs], in_=e2[:, hs], func=ACTF.Copy, scale=r2c[:, h : h + 1])
-            live[("na", g)] = na
+
+        def finish_vector(g):
+            for h, hs in halves(NSC, 2 * GS):
+                nc.vector.tensor_scalar(
+                    out=live[("na", g)][:, hs], in0=live[("e2", g)][:, hs],
+                    scalar1=live[("r2c", g)][:, h : h + 1], scalar2=None, op0=ALU.mult,
+                )
 
         def finish_butterfly(g):
-            sa = scalar_slots(g)
-            e2 = live[("e2", g)]
             na = live[("na", g)]
             o_t = work.tile([P, GS * E], F32, tag="o")
             o4 = o_t[:].rearrange("p (s j e) -> p s j e", j=HALF, e=2)
-            if sa < GS:
-                npl = work.tile([P, (GS - sa) * E], F32, tag="npl")
-                nc.gpsimd.tensor_tensor(
-                    out=npl[:].rearrange("p (g j) -> p g j", j=HALF),
-                    in0=e2[:, sa * E :].rearrange("p (g j) -> p g j", j=HALF),
-                    in1=live[("r2c", g, 1)][:].unsqueeze(2).to_broadcast([P, 2 * (GS - sa), HALF]),
-                    op=ALU.mult,
-                )
-                pieces = ((nc.gpsimd, na[:], 0, sa), (nc.gpsimd, npl[:], sa, GS))
+            if g < NG - TAIL:
+                pieces = ((nc.gpsimd, na[:], 0, GS),)
             else:
                 pieces = (
-                    (nc.vector, na[:, : 2 * E], 0, 2),
-                    (nc.gpsimd, na[:, 2 * E :], 2, GS),
+                    (nc.vector, na[:, 2 * E :], 2, GS),
+                    (nc.gpsimd, na[:, : 2 * E], 0, 2),
                 )
             for eng, src, lo, hi in pieces:
                 nv = src.rearrange("p (s h j) -> p s h j", h=2, j=HALF)
@@ -317,31 +309,33 @@ def tile_waveletmultiheadattention_t_kernel(tc, x, W_q, b_q, W_k, b_k, W_v, b_v,
             if ok(i + 3):
                 transposes(i + 3)
             if ok(i - 4):
-                recip2(i - 4, 1)
-                finish_scalar(i - 4)
+                finish_vector(i - 4)
                 finish_butterfly(i - 4)
+            if ok(i - 1):
+                exp1(i - 1, 0, 2 * GS)
             if ok(i + 2):
                 evacuate(i + 2)
             if ok(i):
                 bias_add(i, 0)
                 bias_add(i, 1)
                 neg_max(i, 0)
-                neg_max(i, 1)
             if ok(i - 1):
                 recip1(i - 1)
+            if ok(i):
+                neg_max(i, 1)
             if ok(i - 3):
-                recip2(i - 3, 0)
+                recip2(i - 3)
+            if ok(i - 1):
+                add_v(i - 1)
             if ok(i + 2):
                 quantise(i + 2)
             if i == -1:
                 prepare_biases()
             if ok(i - 2):
                 exp2(i - 2)
-            if ok(i):
-                exp1(i, 0, 2)
+            if ok(i - 3):
+                finish_scalar(i - 3, 0, 2)
             if ok(i - 2):
                 scale_sums(i - 2)
-            if ok(i):
-                exp1(i, 2, 2 * GS)
-            if ok(i - 1):
-                add_v(i - 1)
+            if ok(i - 3):
+                finish_scalar(i - 3, 2, NSC)

@@ -23,7 +23,7 @@ NG = SLOTS // GS
 CH = 8
 NCH = SLOTS // CH
 C = 0.7071067811865476
-NSC = 7
+NSC = 5
 LEAD = 4
 TAIL = 3
 
@@ -257,6 +257,9 @@ def tile_waveletmultiheadattention_t_kernel(tc, x, W_q, b_q, W_k, b_k, W_v, b_v,
             nc.vector.reciprocal(out=r2c[:], in_=live[("s2c", g)][:])
             live[("r2c", g)] = r2c
 
+        def scalar_halves(g):
+            return NSC if g < NG - TAIL else 0
+
         def finish_scalar(g, lo, hi):
             if lo == 0:
                 na_new = work.tile([P, GS * E], F32, tag="na")
@@ -264,11 +267,11 @@ def tile_waveletmultiheadattention_t_kernel(tc, x, W_q, b_q, W_k, b_k, W_v, b_v,
             e2 = live[("e2", g)]
             r2c = live[("r2c", g)]
             na = live[("na", g)]
-            for h, hs in halves(lo, hi):
+            for h, hs in halves(lo, min(hi, scalar_halves(g))):
                 nc.scalar.activation(out=na[:, hs], in_=e2[:, hs], func=ACTF.Copy, scale=r2c[:, h : h + 1])
 
         def finish_vector(g):
-            for h, hs in halves(NSC, 2 * GS):
+            for h, hs in halves(scalar_halves(g), 2 * GS):
                 nc.vector.tensor_scalar(
                     out=live[("na", g)][:, hs], in0=live[("e2", g)][:, hs],
                     scalar1=live[("r2c", g)][:, h : h + 1], scalar2=None, op0=ALU.mult,
@@ -338,4 +341,4 @@ def tile_waveletmultiheadattention_t_kernel(tc, x, W_q, b_q, W_k, b_k, W_v, b_v,
             if ok(i - 2):
                 scale_sums(i - 2)
             if ok(i - 3):
-                finish_scalar(i - 3, 2, NSC)
+                finish_scalar(i - 3, 2, 2 * GS)

@@ -23,7 +23,7 @@ NG = SLOTS // GS
 CH = 8
 NCH = SLOTS // CH
 C = 0.7071067811865476
-NSC = 5
+NSC = 8
 LEAD = 4
 TAIL = 3
 
@@ -260,41 +260,47 @@ def tile_waveletmultiheadattention_t_kernel(tc, x, W_q, b_q, W_k, b_k, W_v, b_v,
         def scalar_halves(g):
             return NSC if g < NG - TAIL else 0
 
+        def planes(g):
+            return live[("na", g)][:].rearrange("p (s q j) -> p s q j", q=3, j=HALF)
+
         def finish_scalar(g, lo, hi):
             if lo == 0:
-                na_new = work.tile([P, GS * E], F32, tag="na")
+                na_new = work.tile([P, GS * 3 * HALF], F32, tag="na")
                 live[("na", g)] = na_new
             e2 = live[("e2", g)]
             r2c = live[("r2c", g)]
-            na = live[("na", g)]
             for h, hs in halves(lo, min(hi, scalar_halves(g))):
-                nc.scalar.activation(out=na[:, hs], in_=e2[:, hs], func=ACTF.Copy, scale=r2c[:, h : h + 1])
+                nc.scalar.activation(
+                    out=planes(g)[:, h // 2, 2 * (h % 2), :], in_=e2[:, hs], func=ACTF.Copy,
+                    scale=r2c[:, h : h + 1],
+                )
 
         def finish_vector(g):
             for h, hs in halves(scalar_halves(g), 2 * GS):
                 nc.vector.tensor_scalar(
-                    out=live[("na", g)][:, hs], in0=live[("e2", g)][:, hs],
+                    out=planes(g)[:, h // 2, 2 * (h % 2), :], in0=live[("e2", g)][:, hs],
                     scalar1=live[("r2c", g)][:, h : h + 1], scalar2=None, op0=ALU.mult,
                 )
 
         def finish_butterfly(g):
-            na = live[("na", g)]
+            na3 = planes(g)
             o_t = work.tile([P, GS * E], F32, tag="o")
             o4 = o_t[:].rearrange("p (s j e) -> p s j e", j=HALF, e=2)
             if g < NG - TAIL:
-                pieces = ((nc.gpsimd, na[:], 0, GS),)
+                pieces = ((nc.gpsimd, 0, GS),)
             else:
-                pieces = (
-                    (nc.vector, na[:, 2 * E :], 2, GS),
-                    (nc.gpsimd, na[:, : 2 * E], 0, 2),
+                pieces = ((nc.vector, 2, GS), (nc.gpsimd, 0, 2))
+            for eng, lo, hi in pieces:
+                eng.tensor_scalar(
+                    out=na3[:, lo:hi, 1, :], in0=na3[:, lo:hi, 2, :], scalar1=-1.0, scalar2=0.0,
+                    op0=ALU.mult, op1=ALU.add,
                 )
-            for eng, src, lo, hi in pieces:
-                nv = src.rearrange("p (s h j) -> p s h j", h=2, j=HALF)
+            for eng, lo, hi in pieces:
                 eng.tensor_tensor(
-                    out=o4[:, lo:hi, :, 0], in0=nv[:, :, 0, :], in1=nv[:, :, 1, :], op=ALU.subtract
-                )
-                eng.tensor_tensor(
-                    out=o4[:, lo:hi, :, 1], in0=nv[:, :, 0, :], in1=nv[:, :, 1, :], op=ALU.add
+                    out=o4[:, lo:hi, :, :],
+                    in0=na3[:, lo:hi, 0, :].unsqueeze(3).to_broadcast([P, hi - lo, HALF, 2]),
+                    in1=na3[:, lo:hi, 1:3, :].rearrange("p s e j -> p s j e"),
+                    op=ALU.add,
                 )
             nc.sync.dma_start(
                 out=ov[:, g * GS : (g + 1) * GS, :].rearrange("p t f -> p (t f)"), in_=o_t[:]

@@ -248,59 +248,74 @@ def tile_waveletmultiheadattention_t_kernel(tc, x, W_q, b_q, W_k, b_k, W_v, b_v,
             live[("s2", g)] = s2
 
         def scale_sums(g):
-            s2c = small.tile([P, 2 * GS], F32, tag="s2c")
-            nc.scalar.mul(out=s2c[:], in_=live[("s2", g)][:], mul=1.0 / C)
+            s2c = small.tile([P, 2 * GS + 1], F32, tag="s2c")
+            nc.scalar.mul(out=s2c[:, 0 : 2 * GS], in_=live[("s2", g)][:], mul=1.0 / C)
+            nc.scalar.mul(out=s2c[:, 2 * GS :], in_=live[("s2", g)][:, 1:2], mul=-1.0 / C)
             live[("s2c", g)] = s2c
 
         def recip2(g):
-            r2c = small.tile([P, 2 * GS], F32, tag="r2c")
+            r2c = small.tile([P, 2 * GS + 1], F32, tag="r2c")
             nc.vector.reciprocal(out=r2c[:], in_=live[("s2c", g)][:])
             live[("r2c", g)] = r2c
 
-        def scalar_halves(g):
-            return NSC if g < NG - TAIL else 0
-
         def planes(g):
             return live[("na", g)][:].rearrange("p (s q j) -> p s q j", q=3, j=HALF)
+
+        def in_tail(g):
+            return g >= NG - TAIL
+
+        scalar_jobs = (
+            (0, 2, 1, 1), (0, 1, 1, 8), (1, 0, 2, 2), (1, 2, 3, 3), (2, 0, 4, 4), (2, 2, 5, 5), (3, 0, 6, 6),
+        )
+        vector_jobs = ((3, 2, 7, 7),)
+        tail_jobs = tuple((h // 2, 2 * (h % 2), h, h) for h in range(2 * GS))
 
         def finish_scalar(g, lo, hi):
             if lo == 0:
                 na_new = work.tile([P, GS * 3 * HALF], F32, tag="na")
                 live[("na", g)] = na_new
-            e2 = live[("e2", g)]
-            r2c = live[("r2c", g)]
-            for h, hs in halves(lo, min(hi, scalar_halves(g))):
+            if in_tail(g):
+                return
+            for s, q, h, col in scalar_jobs[lo:hi]:
                 nc.scalar.activation(
-                    out=planes(g)[:, h // 2, 2 * (h % 2), :], in_=e2[:, hs], func=ACTF.Copy,
-                    scale=r2c[:, h : h + 1],
+                    out=planes(g)[:, s, q, :], in_=live[("e2", g)][:, h * HALF : (h + 1) * HALF],
+                    func=ACTF.Copy, scale=live[("r2c", g)][:, col : col + 1],
                 )
 
         def finish_vector(g):
-            for h, hs in halves(scalar_halves(g), 2 * GS):
+            e2 = live[("e2", g)]
+            r2c = live[("r2c", g)]
+            o_t = work.tile([P, GS * E], F32, tag="o")
+            live[("o", g)] = o_t
+            if not in_tail(g):
+                nc.vector.scalar_tensor_tensor(
+                    out=o_t[:, 0:E].rearrange("p (j e) -> p j e", e=2),
+                    in0=e2[:, 0:HALF].unsqueeze(2).to_broadcast([P, HALF, 2]),
+                    scalar=r2c[:, 0:1],
+                    in1=planes(g)[:, 0, 1:3, :].rearrange("p e j -> p j e"),
+                    op0=ALU.mult,
+                    op1=ALU.add,
+                )
+            for s, q, h, col in tail_jobs if in_tail(g) else vector_jobs:
                 nc.vector.tensor_scalar(
-                    out=planes(g)[:, h // 2, 2 * (h % 2), :], in0=live[("e2", g)][:, hs],
-                    scalar1=live[("r2c", g)][:, h : h + 1], scalar2=None, op0=ALU.mult,
+                    out=planes(g)[:, s, q, :], in0=e2[:, h * HALF : (h + 1) * HALF],
+                    scalar1=r2c[:, col : col + 1], scalar2=None, op0=ALU.mult,
                 )
 
         def finish_butterfly(g):
             na3 = planes(g)
-            o_t = work.tile([P, GS * E], F32, tag="o")
+            o_t = live[("o", g)]
             o4 = o_t[:].rearrange("p (s j e) -> p s j e", j=HALF, e=2)
-            if g < NG - TAIL:
-                pieces = ((nc.gpsimd, 0, GS),)
-            else:
+            if in_tail(g):
                 pieces = ((nc.vector, 2, GS), (nc.gpsimd, 0, 2))
-            for eng, lo, hi in pieces:
-                eng.tensor_scalar(
-                    out=na3[:, lo:hi, 1, :], in0=na3[:, lo:hi, 2, :], scalar1=-1.0, scalar2=0.0,
-                    op0=ALU.mult, op1=ALU.add,
-                )
+            else:
+                pieces = ((nc.gpsimd, 1, GS),)
             for eng, lo, hi in pieces:
                 eng.tensor_tensor(
-                    out=o4[:, lo:hi, :, :],
-                    in0=na3[:, lo:hi, 0, :].unsqueeze(3).to_broadcast([P, hi - lo, HALF, 2]),
-                    in1=na3[:, lo:hi, 1:3, :].rearrange("p s e j -> p s j e"),
-                    op=ALU.add,
+                    out=o4[:, lo:hi, :, 0], in0=na3[:, lo:hi, 0, :], in1=na3[:, lo:hi, 2, :], op=ALU.subtract
+                )
+                eng.tensor_tensor(
+                    out=o4[:, lo:hi, :, 1], in0=na3[:, lo:hi, 0, :], in1=na3[:, lo:hi, 2, :], op=ALU.add
                 )
             nc.sync.dma_start(
                 out=ov[:, g * GS : (g + 1) * GS, :].rearrange("p t f -> p (t f)"), in_=o_t[:]

@@ -19,13 +19,16 @@ HALF = 64
 TOKENS = 4 * 4096
 SLOTS = TOKENS // P
 GS = 4
-NG = SLOTS // GS
+SIZES = (2, 2) + (GS,) * 30 + (2, 2)
+NG = len(SIZES)
+STARTS = tuple(sum(SIZES[:g]) for g in range(NG))
 CH = 8
 NCH = SLOTS // CH
 C = 0.7071067811865476
-NSC = 8
 LEAD = 4
 TAIL = 3
+
+assert sum(SIZES) == SLOTS
 
 FLOPS = 2 * TOKENS * D * 3 * E
 
@@ -48,27 +51,27 @@ def tile_waveletmultiheadattention_t_kernel(tc, x, W_q, b_q, W_k, b_k, W_v, b_v,
 
         live = {}
 
-        def load(c):
+        def load(c, cuts):
             x_sb = xpool.tile([P, CH * D], BF16, tag="x")
-            nc.sync.dma_start(
-                out=x_sb[:], in_=xv[:, c * CH : (c + 1) * CH, :].rearrange("p t k -> p (t k)")
-            )
+            for lo, hi in cuts:
+                nc.sync.dma_start(
+                    out=x_sb[:, lo * D : hi * D],
+                    in_=xv[:, c * CH + lo : c * CH + hi, :].rearrange("p t k -> p (t k)"),
+                )
             live[("x", c)] = x_sb
 
         w_sb = const.tile([P, 3 * D], BF16)
         for i, w in enumerate((W_q, W_k, W_v)):
             nc.sync.dma_start(out=w_sb[:, i * D : (i + 1) * D], in_=w)
-        x_first = xpool.tile([P, CH * D], BF16, tag="x")
-        for hf in range(2):
-            nc.sync.dma_start(
-                out=x_first[:, hf * GS * D : (hf + 1) * GS * D],
-                in_=xv[:, hf * GS : (hf + 1) * GS, :].rearrange("p t k -> p (t k)"),
-            )
-        live[("x", 0)] = x_first
-        load(1)
-        bb = const.tile([P, 3, E], BF16)
-        for i, b in enumerate((b_q, b_k, b_v)):
-            nc.scalar.dma_start(out=bb[:, i, :], in_=b.partition_broadcast(P))
+        load(0, ((0, 2), (2, 4), (4, 8)))
+        load(1, ((0, CH),))
+        brow = const.tile([P, 2 * E], BF16)
+        ones = const.tile([P, P], BF16)
+        nc.vector.memset(brow[:], 0.0)
+        nc.vector.memset(ones[:], 1.0)
+        nc.scalar.dma_start(out=brow[0:1, 0:E], in_=b_q.unsqueeze(0))
+        nc.scalar.dma_start(out=brow[1:2, 0:E], in_=b_k.unsqueeze(0))
+        nc.scalar.dma_start(out=brow[0:1, E : 2 * E], in_=b_v.unsqueeze(0))
 
         ident = const.tile([P, P], F32)
         make_identity(nc, ident[:])
@@ -81,60 +84,58 @@ def tile_waveletmultiheadattention_t_kernel(tc, x, W_q, b_q, W_k, b_k, W_v, b_v,
         ww = w_sb[:].bitcast(F32)
         wg = const.tile([P, 6 * E * 4], BF16, align_bytes=64)
         wgf = wg[:].bitcast(F32).rearrange("p (w q h j u) -> p w q h j u", w=3, q=2, h=2, u=2)
-        wgw = wg[:].bitcast(F32).rearrange("p (w q h c) -> p w q h c", w=3, q=2, h=2)
         wgb = wg[:].rearrange("p (w q h c) -> p w q h c", w=3, q=2, h=2)
+        wcodes = const.tile([P, 6 * E], U32, align_bytes=64)
+        wscales = const.tile([P, 6 * E], U8, align_bytes=64)
+
+        def negate_even(i):
+            nc.vector.tensor_scalar(
+                out=wgb[:, i, 0, 1, :], in0=wgb[:, i, 0, 0, :], scalar1=-1.0, scalar2=None, op0=ALU.mult
+            )
+
+        def quantise_weights(lo, hi):
+            nc.vector.quantize_mx(
+                out=wcodes[:, lo:hi].bitcast(FP8X4), scales=wscales[:, lo:hi], in_=wg[:, 4 * lo : 4 * hi]
+            )
+
         for i in range(3):
             wt = psx.tile([P, 512], F32, tag="xt")
             for u in range(2):
                 nc.tensor.transpose(
                     wt[:, u * P : (u + 1) * P], ww[:, i * 256 + u * P : i * 256 + (u + 1) * P], ident[:]
                 )
+            wtv = wt[:, 0:256].rearrange("p (u j q) -> p q j u", u=2, q=2)
+            nc.vector.tensor_copy(out=wgf[:, i, 0, 0, :, :], in_=wtv[:, 0, :, :])
+            if i > 0:
+                negate_even(i - 1)
             nc.vector.tensor_copy(
-                out=wgf[:, i, :, 0, :, :],
-                in_=wt[:, 0:256].rearrange("p (u j q) -> p q j u", u=2, q=2),
+                out=wgf[:, i, 1, :, :, :], in_=wtv[:, 1, :, :].unsqueeze(1).to_broadcast([P, 2, HALF, 2])
             )
-        nc.vector.tensor_copy(out=wgw[:, :, 1, 1, :], in_=wgw[:, :, 1, 0, :])
-        nc.vector.tensor_scalar(
-            out=wgb[:, :, 0, 1, :], in0=wgb[:, :, 0, 0, :], scalar1=-1.0, scalar2=None, op0=ALU.mult
-        )
-        wcodes = const.tile([P, 6 * E], U32, align_bytes=64)
-        wscales = const.tile([P, 6 * E], U8, align_bytes=64)
-        nc.vector.quantize_mx(
-            out=wcodes[:, 0:512].bitcast(FP8X4), scales=wscales[:, 0:512], in_=wg[:, 0:2048]
-        )
-        nc.vector.quantize_mx(
-            out=wcodes[:, 512:768].bitcast(FP8X4), scales=wscales[:, 512:768], in_=wg[:, 2048:3072]
-        )
+        quantise_weights(0, 512)
+        negate_even(2)
 
+        b_ps = pst.tile([P, GS * E], F32, tag="V")
+        nc.tensor.matmul(out=b_ps[:, 0 : 2 * E], lhsT=ones[:], rhs=brow[:], start=True, stop=True)
+        bs = const.tile([P, 2 * E], F32)
+        nc.scalar.mul(out=bs[:], in_=b_ps[:, 0 : 2 * E], mul=C)
         bh = const.tile([P, 2, E], F32)
 
         def prepare_biases():
-            bs = const.tile([P, 2, E], F32)
-            nc.vector.tensor_tensor(out=bs[:, 0, :], in0=bb[:, 0, :], in1=bb[:, 1, :], op=ALU.add)
-            nc.vector.tensor_copy(out=bs[:, 1, :], in_=bb[:, 2, :])
-            bsv = bs[:].rearrange("p a (j q) -> p a j q", q=2)
-            bh0 = const.tile([P, 2, 2, HALF], F32)
+            bsv = bs[:].rearrange("p (a j q) -> p a j q", a=2, q=2)
             nc.vector.tensor_tensor(
-                out=bh0[:, :, 0, :], in0=bsv[:, :, :, 0], in1=bsv[:, :, :, 1], op=ALU.add
+                out=bh[:, :, 0:HALF], in0=bsv[:, :, :, 0], in1=bsv[:, :, :, 1], op=ALU.add
             )
             nc.vector.tensor_tensor(
-                out=bh0[:, :, 1, :], in0=bsv[:, :, :, 1], in1=bsv[:, :, :, 0], op=ALU.subtract
-            )
-            nc.vector.tensor_scalar(
-                out=bh[:].rearrange("p a f -> p (a f)"),
-                in0=bh0[:].rearrange("p a h j -> p (a h j)"),
-                scalar1=C,
-                scalar2=None,
-                op0=ALU.mult,
+                out=bh[:, :, HALF:E], in0=bsv[:, :, :, 1], in1=bsv[:, :, :, 0], op=ALU.subtract
             )
 
         def halves(lo, hi):
             return [(h, slice(h * HALF, (h + 1) * HALF)) for h in range(lo, hi)]
 
         def transposes(g):
-            xw = live[("x", g // 2)][:].bitcast(F32)
-            base = (g % 2) * 1024
-            for b in range(2):
+            xw = live[("x", STARTS[g] // CH)][:].bitcast(F32)
+            base = (STARTS[g] % CH) * 256
+            for b in range(SIZES[g] // 2):
                 xt = psx.tile([P, 512], F32, tag="xt")
                 for i in range(4):
                     o = base + b * 512 + i * P
@@ -144,7 +145,7 @@ def tile_waveletmultiheadattention_t_kernel(tc, x, W_q, b_q, W_k, b_k, W_v, b_v,
         def evacuate(g):
             grouped = gpool.tile([P, GS * P * 4], BF16, tag="grouped", align_bytes=64)
             gf = grouped[:].bitcast(F32)
-            for b in range(2):
+            for b in range(SIZES[g] // 2):
                 nc.scalar.copy(
                     out=gf[:, b * 512 : (b + 1) * 512].rearrange("p (s r u) -> p s r u", s=2, u=2),
                     in_=live[("xt", g, b)][:].rearrange("p (s u r) -> p s r u", s=2, u=2),
@@ -152,10 +153,11 @@ def tile_waveletmultiheadattention_t_kernel(tc, x, W_q, b_q, W_k, b_k, W_v, b_v,
             live[("grouped", g)] = grouped
 
         def quantise(g):
+            n = SIZES[g] * P
             codes = qpool.tile([P, GS * P], U32, tag="codes", align_bytes=64)
             scales = qpool.tile([P, GS * P], U8, tag="scales", align_bytes=64)
             nc.vector.quantize_mx(
-                out=codes[:].bitcast(FP8X4), scales=scales[:], in_=live[("grouped", g)][:]
+                out=codes[:, 0:n].bitcast(FP8X4), scales=scales[:, 0:n], in_=live[("grouped", g)][:, 0 : 4 * n]
             )
             live[("codes", g)] = codes
             live[("scales", g)] = scales
@@ -166,7 +168,7 @@ def tile_waveletmultiheadattention_t_kernel(tc, x, W_q, b_q, W_k, b_k, W_v, b_v,
             t_ps = pst.tile([P, GS * E], F32, tag="T")
             v_ps = pst.tile([P, GS * E], F32, tag="V")
             for dst, blks in ((t_ps, (0, 1, 2, 3)), (v_ps, (4, 5))):
-                for s in range(GS):
+                for s in range(SIZES[g]):
                     cs = slice(s * P, (s + 1) * P)
                     for n, blk in enumerate(blks):
                         nc.tensor.matmul_mx(
@@ -182,44 +184,45 @@ def tile_waveletmultiheadattention_t_kernel(tc, x, W_q, b_q, W_k, b_k, W_v, b_v,
             live[("ps", g, 1)] = v_ps
 
         def bias_add(g, a):
+            n = SIZES[g]
             dst = work.tile([P, GS * E], F32, tag="uv%d" % a, name="uv%d" % a)
             nc.vector.scalar_tensor_tensor(
-                out=dst[:].rearrange("p (s f) -> p s f", f=E),
-                in0=live[("ps", g, a)][:].rearrange("p (s f) -> p s f", f=E),
+                out=dst[:, 0 : n * E].rearrange("p (s f) -> p s f", f=E),
+                in0=live[("ps", g, a)][:, 0 : n * E].rearrange("p (s f) -> p s f", f=E),
                 scalar=C,
-                in1=bh[:, a, :].unsqueeze(1).to_broadcast([P, GS, E]),
+                in1=bh[:, a, :].unsqueeze(1).to_broadcast([P, n, E]),
                 op0=ALU.mult,
                 op1=ALU.add,
             )
             live[("uv", g, a)] = dst
 
         def neg_max(g, a):
+            n = SIZES[g]
             nm = small.tile([P, 2 * GS], F32, tag="nm%d" % a, name="nm%d" % a)
             nc.vector.tensor_reduce(
-                out=nm[:], in_=live[("uv", g, a)][:].rearrange("p (g j) -> p g j", j=HALF), axis=AX.X,
-                op=ALU.max, negate=True,
+                out=nm[:, 0 : 2 * n],
+                in_=live[("uv", g, a)][:, 0 : n * E].rearrange("p (g j) -> p g j", j=HALF),
+                axis=AX.X, op=ALU.max, negate=True,
             )
             live[("nm", g, a)] = nm
 
-        def exp1(g, lo, hi):
-            if lo == 0:
-                e1_new = work.tile([P, GS * E], F32, tag="e1")
-                s1_new = small.tile([P, 2 * GS], F32, tag="s1")
-                live[("e1", g)] = e1_new
-                live[("s1", g)] = s1_new
-            e1 = live[("e1", g)]
-            s1 = live[("s1", g)]
+        def exp1(g):
+            e1 = work.tile([P, GS * E], F32, tag="e1")
+            s1 = small.tile([P, 2 * GS], F32, tag="s1")
             u_sb = live[("uv", g, 0)]
             nm1 = live[("nm", g, 0)]
-            for h, hs in halves(lo, hi):
+            for h, hs in halves(0, 2 * SIZES[g]):
                 nc.scalar.activation(
                     out=e1[:, hs], in_=u_sb[:, hs], func=ACTF.Exp, bias=nm1[:, h : h + 1], scale=1.0,
                     accum_out=s1[:, h : h + 1],
                 )
+            live[("e1", g)] = e1
+            live[("s1", g)] = s1
 
         def recip1(g):
+            n2 = 2 * SIZES[g]
             r1 = small.tile([P, 2 * GS], F32, tag="r1")
-            nc.vector.reciprocal(out=r1[:], in_=live[("s1", g)][:])
+            nc.vector.reciprocal(out=r1[:, 0:n2], in_=live[("s1", g)][:, 0:n2])
             live[("r1", g)] = r1
 
         def add_v(g):
@@ -227,7 +230,7 @@ def tile_waveletmultiheadattention_t_kernel(tc, x, W_q, b_q, W_k, b_k, W_v, b_v,
             e1 = live[("e1", g)]
             r1 = live[("r1", g)]
             vb_sb = live[("uv", g, 1)]
-            for h, hs in halves(0, 2 * GS):
+            for h, hs in halves(0, 2 * SIZES[g]):
                 nc.vector.scalar_tensor_tensor(
                     out=w_t[:, hs], in0=e1[:, hs], scalar=r1[:, h : h + 1], in1=vb_sb[:, hs],
                     op0=ALU.mult, op1=ALU.add,
@@ -239,7 +242,7 @@ def tile_waveletmultiheadattention_t_kernel(tc, x, W_q, b_q, W_k, b_k, W_v, b_v,
             s2 = small.tile([P, 2 * GS], F32, tag="s2")
             w_t = live[("w", g)]
             nm2 = live[("nm", g, 1)]
-            for h, hs in halves(0, 2 * GS):
+            for h, hs in halves(0, 2 * SIZES[g]):
                 nc.scalar.activation(
                     out=e2[:, hs], in_=w_t[:, hs], func=ACTF.Exp, bias=nm2[:, h : h + 1], scale=1.0,
                     accum_out=s2[:, h : h + 1],
@@ -248,86 +251,64 @@ def tile_waveletmultiheadattention_t_kernel(tc, x, W_q, b_q, W_k, b_k, W_v, b_v,
             live[("s2", g)] = s2
 
         def scale_sums(g):
-            s2c = small.tile([P, 2 * GS + 1], F32, tag="s2c")
-            nc.scalar.mul(out=s2c[:, 0 : 2 * GS], in_=live[("s2", g)][:], mul=1.0 / C)
-            nc.scalar.mul(out=s2c[:, 2 * GS :], in_=live[("s2", g)][:, 1:2], mul=-1.0 / C)
+            n2 = 2 * SIZES[g]
+            s2c = small.tile([P, 2 * GS], F32, tag="s2c")
+            nc.scalar.mul(out=s2c[:, 0:n2], in_=live[("s2", g)][:, 0:n2], mul=1.0 / C)
             live[("s2c", g)] = s2c
 
         def recip2(g):
-            r2c = small.tile([P, 2 * GS + 1], F32, tag="r2c")
-            nc.vector.reciprocal(out=r2c[:], in_=live[("s2c", g)][:])
+            n2 = 2 * SIZES[g]
+            r2c = small.tile([P, 2 * GS], F32, tag="r2c")
+            nc.vector.reciprocal(out=r2c[:, 0:n2], in_=live[("s2c", g)][:, 0:n2])
             live[("r2c", g)] = r2c
 
-        def planes(g):
-            return live[("na", g)][:].rearrange("p (s q j) -> p s q j", q=3, j=HALF)
-
-        def in_tail(g):
-            return g >= NG - TAIL
-
-        scalar_jobs = (
-            (0, 2, 1, 1), (0, 1, 1, 8), (1, 0, 2, 2), (1, 2, 3, 3), (2, 0, 4, 4), (2, 2, 5, 5), (3, 0, 6, 6),
-        )
-        vector_jobs = ((3, 2, 7, 7),)
-        tail_jobs = tuple((h // 2, 2 * (h % 2), h, h) for h in range(2 * GS))
+        def scalar_halves(g):
+            return 2 * SIZES[g] - 1 if g < NG - TAIL else 0
 
         def finish_scalar(g, lo, hi):
             if lo == 0:
-                na_new = work.tile([P, GS * 3 * HALF], F32, tag="na")
+                na_new = work.tile([P, GS * E], F32, tag="na")
                 live[("na", g)] = na_new
-            if in_tail(g):
-                return
-            for s, q, h, col in scalar_jobs[lo:hi]:
-                nc.scalar.activation(
-                    out=planes(g)[:, s, q, :], in_=live[("e2", g)][:, h * HALF : (h + 1) * HALF],
-                    func=ACTF.Copy, scale=live[("r2c", g)][:, col : col + 1],
-                )
-
-        def finish_vector(g):
             e2 = live[("e2", g)]
             r2c = live[("r2c", g)]
-            o_t = work.tile([P, GS * E], F32, tag="o")
-            live[("o", g)] = o_t
-            if not in_tail(g):
-                nc.vector.scalar_tensor_tensor(
-                    out=o_t[:, 0:E].rearrange("p (j e) -> p j e", e=2),
-                    in0=e2[:, 0:HALF].unsqueeze(2).to_broadcast([P, HALF, 2]),
-                    scalar=r2c[:, 0:1],
-                    in1=planes(g)[:, 0, 1:3, :].rearrange("p e j -> p j e"),
-                    op0=ALU.mult,
-                    op1=ALU.add,
-                )
-            for s, q, h, col in tail_jobs if in_tail(g) else vector_jobs:
+            na = live[("na", g)]
+            for h, hs in halves(lo, min(hi, scalar_halves(g))):
+                nc.scalar.activation(out=na[:, hs], in_=e2[:, hs], func=ACTF.Copy, scale=r2c[:, h : h + 1])
+
+        def finish_vector(g):
+            for h, hs in halves(scalar_halves(g), 2 * SIZES[g]):
                 nc.vector.tensor_scalar(
-                    out=planes(g)[:, s, q, :], in0=e2[:, h * HALF : (h + 1) * HALF],
-                    scalar1=r2c[:, col : col + 1], scalar2=None, op0=ALU.mult,
+                    out=live[("na", g)][:, hs], in0=live[("e2", g)][:, hs],
+                    scalar1=live[("r2c", g)][:, h : h + 1], scalar2=None, op0=ALU.mult,
                 )
 
         def finish_butterfly(g):
-            na3 = planes(g)
-            o_t = live[("o", g)]
+            n = SIZES[g]
+            nv = live[("na", g)][:].rearrange("p (s h j) -> p s h j", h=2, j=HALF)
+            o_t = work.tile([P, GS * E], F32, tag="o")
             o4 = o_t[:].rearrange("p (s j e) -> p s j e", j=HALF, e=2)
-            if in_tail(g):
-                pieces = ((nc.vector, 2, GS), (nc.gpsimd, 0, 2))
+            if g < NG - TAIL:
+                pieces = ((nc.gpsimd, 0, n),)
             else:
-                pieces = ((nc.gpsimd, 1, GS),)
+                pieces = ((nc.vector, n // 2, n), (nc.gpsimd, 0, n // 2))
             for eng, lo, hi in pieces:
                 eng.tensor_tensor(
-                    out=o4[:, lo:hi, :, 0], in0=na3[:, lo:hi, 0, :], in1=na3[:, lo:hi, 2, :], op=ALU.subtract
+                    out=o4[:, lo:hi, :, 0], in0=nv[:, lo:hi, 0, :], in1=nv[:, lo:hi, 1, :], op=ALU.subtract
                 )
                 eng.tensor_tensor(
-                    out=o4[:, lo:hi, :, 1], in0=na3[:, lo:hi, 0, :], in1=na3[:, lo:hi, 2, :], op=ALU.add
+                    out=o4[:, lo:hi, :, 1], in0=nv[:, lo:hi, 0, :], in1=nv[:, lo:hi, 1, :], op=ALU.add
                 )
             nc.sync.dma_start(
-                out=ov[:, g * GS : (g + 1) * GS, :].rearrange("p t f -> p (t f)"), in_=o_t[:]
+                out=ov[:, STARTS[g] : STARTS[g] + n, :].rearrange("p t f -> p (t f)"), in_=o_t[:, 0 : n * E]
             )
 
         def ok(g):
             return 0 <= g < NG
 
         for i in range(-3, NG + 4):
-            nxt = i + 3 + LEAD
-            if nxt % 2 == 0 and 2 <= nxt // 2 < NCH:
-                load(nxt // 2)
+            ahead = i + 3 + LEAD
+            if ok(ahead) and STARTS[ahead] % CH == 0 and STARTS[ahead] // CH >= 2:
+                load(STARTS[ahead] // CH, ((0, CH),))
             if ok(i + 1):
                 passes(i + 1)
             if ok(i + 3):
@@ -336,7 +317,7 @@ def tile_waveletmultiheadattention_t_kernel(tc, x, W_q, b_q, W_k, b_k, W_v, b_v,
                 finish_vector(i - 4)
                 finish_butterfly(i - 4)
             if ok(i - 1):
-                exp1(i - 1, 0, 2 * GS)
+                exp1(i - 1)
             if ok(i + 2):
                 evacuate(i + 2)
             if ok(i):
@@ -353,6 +334,8 @@ def tile_waveletmultiheadattention_t_kernel(tc, x, W_q, b_q, W_k, b_k, W_v, b_v,
                 add_v(i - 1)
             if ok(i + 2):
                 quantise(i + 2)
+            if i == -2:
+                quantise_weights(512, 768)
             if i == -1:
                 prepare_biases()
             if ok(i - 2):

@@ -105,12 +105,16 @@ def tile_waveletmultiheadattention_t_kernel(tc, x, W_q, b_q, W_k, b_k, W_v, b_v,
                     wt[:, u * P : (u + 1) * P], ww[:, i * 256 + u * P : i * 256 + (u + 1) * P], ident[:]
                 )
             wtv = wt[:, 0:256].rearrange("p (u j q) -> p q j u", u=2, q=2)
-            nc.vector.tensor_copy(out=wgf[:, i, 0, 0, :, :], in_=wtv[:, 0, :, :])
-            if i > 0:
-                negate_even(i - 1)
-            nc.vector.tensor_copy(
-                out=wgf[:, i, 1, :, :, :], in_=wtv[:, 1, :, :].unsqueeze(1).to_broadcast([P, 2, HALF, 2])
-            )
+            odd_twice = wtv[:, 1, :, :].unsqueeze(1).to_broadcast([P, 2, HALF, 2])
+            if i == 1:
+                nc.scalar.copy(out=wgf[:, i, 0, 0, :, :], in_=wtv[:, 0, :, :])
+                nc.scalar.copy(out=wgf[:, i, 1, :, :, :], in_=odd_twice)
+            else:
+                nc.vector.tensor_copy(out=wgf[:, i, 0, 0, :, :], in_=wtv[:, 0, :, :])
+                if i == 2:
+                    negate_even(0)
+                    negate_even(1)
+                nc.vector.tensor_copy(out=wgf[:, i, 1, :, :, :], in_=odd_twice)
         quantise_weights(0, 512)
         negate_even(2)
 
@@ -263,7 +267,7 @@ def tile_waveletmultiheadattention_t_kernel(tc, x, W_q, b_q, W_k, b_k, W_v, b_v,
             live[("r2c", g)] = r2c
 
         def scalar_halves(g):
-            return 2 * SIZES[g] - 1 if g < NG - TAIL else 0
+            return 2 * SIZES[g] if g < NG - TAIL else 0
 
         def finish_scalar(g, lo, hi):
             if lo == 0:

from contextlib import ExitStack

import concourse.mybir as mybir
from concourse.masks import make_identity

F32 = mybir.dt.float32
BF16 = mybir.dt.bfloat16
U32 = mybir.dt.uint32
U8 = mybir.dt.uint8
FP8X4 = mybir.dt.float8_e4m3fn_x4
ALU = mybir.AluOpType
ACTF = mybir.ActivationFunctionType
AX = mybir.AxisListType

P = 128
D = 512
E = 128
HALF = 64
TOKENS = 4 * 4096
SLOTS = TOKENS // P
GS = 4
SIZES = (2, 2) + (GS,) * 30 + (2, 2)
NG = len(SIZES)
STARTS = tuple(sum(SIZES[:g]) for g in range(NG))
CH = 8
NCH = SLOTS // CH
C = 0.7071067811865476
LEAD = 4
TAIL = 3

assert sum(SIZES) == SLOTS

FLOPS = 2 * TOKENS * D * 3 * E


def tile_waveletmultiheadattention_t_kernel(tc, x, W_q, b_q, W_k, b_k, W_v, b_v, out):
    nc = tc.nc
    xv = x.flatten_outer_dims().rearrange("(p t) k -> p t k", p=P)
    ov = out.flatten_outer_dims().rearrange("(p t) f -> p t f", p=P)

    with ExitStack() as ctx:
        const = ctx.enter_context(tc.tile_pool(name="const", bufs=1))
        xpool = ctx.enter_context(tc.tile_pool(name="xpool", bufs=4))
        gpool = ctx.enter_context(tc.tile_pool(name="gpool", bufs=3))
        qpool = ctx.enter_context(tc.tile_pool(name="qpool", bufs=3))
        work = ctx.enter_context(tc.tile_pool(name="work", bufs=4))
        small = ctx.enter_context(tc.tile_pool(name="small", bufs=6))
        psx = ctx.enter_context(tc.psum_pool(name="psx", bufs=4))
        pst = ctx.enter_context(tc.psum_pool(name="pst", bufs=2))
        ctx.enter_context(tc.manual_schedule())

        live = {}

        def load(c, cuts):
            x_sb = xpool.tile([P, CH * D], BF16, tag="x")
            for lo, hi in cuts:
                nc.sync.dma_start(
                    out=x_sb[:, lo * D : hi * D],
                    in_=xv[:, c * CH + lo : c * CH + hi, :].rearrange("p t k -> p (t k)"),
                )
            live[("x", c)] = x_sb

        w_sb = const.tile([P, 3 * D], BF16)
        for i, w in enumerate((W_q, W_k, W_v)):
            nc.sync.dma_start(out=w_sb[:, i * D : (i + 1) * D], in_=w)
        load(0, ((0, 2), (2, 4), (4, 8)))
        load(1, ((0, CH),))
        brow = const.tile([P, 2 * E], BF16)
        ones = const.tile([P, P], BF16)
        nc.vector.memset(brow[:], 0.0)
        nc.vector.memset(ones[:], 1.0)
        nc.scalar.dma_start(out=brow[0:1, 0:E], in_=b_q.unsqueeze(0))
        nc.scalar.dma_start(out=brow[1:2, 0:E], in_=b_k.unsqueeze(0))
        nc.scalar.dma_start(out=brow[0:1, E : 2 * E], in_=b_v.unsqueeze(0))

        ident = const.tile([P, P], F32)
        make_identity(nc, ident[:])

        warm_in = const.tile([P, 1], F32)
        warm_out = const.tile([P, 1], F32)
        nc.vector.memset(warm_in[:], 0.0)
        nc.scalar.activation(out=warm_out[:], in_=warm_in[:], func=ACTF.Exp)

        ww = w_sb[:].bitcast(F32)
        wg = const.tile([P, 6 * E * 4], BF16, align_bytes=64)
        wgf = wg[:].bitcast(F32).rearrange("p (w q h j u) -> p w q h j u", w=3, q=2, h=2, u=2)
        wgb = wg[:].rearrange("p (w q h c) -> p w q h c", w=3, q=2, h=2)
        wcodes = const.tile([P, 6 * E], U32, align_bytes=64)
        wscales = const.tile([P, 6 * E], U8, align_bytes=64)

        def negate_even(i):
            nc.vector.tensor_scalar(
                out=wgb[:, i, 0, 1, :], in0=wgb[:, i, 0, 0, :], scalar1=-1.0, scalar2=None, op0=ALU.mult
            )

        def quantise_weights(lo, hi):
            nc.vector.quantize_mx(
                out=wcodes[:, lo:hi].bitcast(FP8X4), scales=wscales[:, lo:hi], in_=wg[:, 4 * lo : 4 * hi]
            )

        for i in range(3):
            wt = psx.tile([P, 512], F32, tag="xt")
            for u in range(2):
                nc.tensor.transpose(
                    wt[:, u * P : (u + 1) * P], ww[:, i * 256 + u * P : i * 256 + (u + 1) * P], ident[:]
                )
            wtv = wt[:, 0:256].rearrange("p (u j q) -> p q j u", u=2, q=2)
            odd_twice = wtv[:, 1, :, :].unsqueeze(1).to_broadcast([P, 2, HALF, 2])
            if i == 1:
                nc.scalar.copy(out=wgf[:, i, 0, 0, :, :], in_=wtv[:, 0, :, :])
                nc.scalar.copy(out=wgf[:, i, 1, :, :, :], in_=odd_twice)
            else:
                nc.vector.tensor_copy(out=wgf[:, i, 0, 0, :, :], in_=wtv[:, 0, :, :])
                if i == 2:
                    negate_even(0)
                    negate_even(1)
                nc.vector.tensor_copy(out=wgf[:, i, 1, :, :, :], in_=odd_twice)
        quantise_weights(0, 512)
        negate_even(2)

        b_ps = pst.tile([P, GS * E], F32, tag="V")
        nc.tensor.matmul(out=b_ps[:, 0 : 2 * E], lhsT=ones[:], rhs=brow[:], start=True, stop=True)
        bs = const.tile([P, 2 * E], F32)
        nc.scalar.mul(out=bs[:], in_=b_ps[:, 0 : 2 * E], mul=C)
        bh = const.tile([P, 2, E], F32)

        def prepare_biases():
            bsv = bs[:].rearrange("p (a j q) -> p a j q", a=2, q=2)
            nc.vector.tensor_tensor(
                out=bh[:, :, 0:HALF], in0=bsv[:, :, :, 0], in1=bsv[:, :, :, 1], op=ALU.add
            )
            nc.vector.tensor_tensor(
                out=bh[:, :, HALF:E], in0=bsv[:, :, :, 1], in1=bsv[:, :, :, 0], op=ALU.subtract
            )

        def halves(lo, hi):
            return [(h, slice(h * HALF, (h + 1) * HALF)) for h in range(lo, hi)]

        def transposes(g):
            xw = live[("x", STARTS[g] // CH)][:].bitcast(F32)
            base = (STARTS[g] % CH) * 256
            for b in range(SIZES[g] // 2):
                xt = psx.tile([P, 512], F32, tag="xt")
                for i in range(4):
                    o = base + b * 512 + i * P
                    nc.tensor.transpose(xt[:, i * P : (i + 1) * P], xw[:, o : o + P], ident[:])
                live[("xt", g, b)] = xt

        def evacuate(g):
            grouped = gpool.tile([P, GS * P * 4], BF16, tag="grouped", align_bytes=64)
            gf = grouped[:].bitcast(F32)
            for b in range(SIZES[g] // 2):
                nc.scalar.copy(
                    out=gf[:, b * 512 : (b + 1) * 512].rearrange("p (s r u) -> p s r u", s=2, u=2),
                    in_=live[("xt", g, b)][:].rearrange("p (s u r) -> p s r u", s=2, u=2),
                )
            live[("grouped", g)] = grouped

        def quantise(g):
            n = SIZES[g] * P
            codes = qpool.tile([P, GS * P], U32, tag="codes", align_bytes=64)
            scales = qpool.tile([P, GS * P], U8, tag="scales", align_bytes=64)
            nc.vector.quantize_mx(
                out=codes[:, 0:n].bitcast(FP8X4), scales=scales[:, 0:n], in_=live[("grouped", g)][:, 0 : 4 * n]
            )
            live[("codes", g)] = codes
            live[("scales", g)] = scales

        def passes(g):
            codes = live[("codes", g)]
            scales = live[("scales", g)]
            t_ps = pst.tile([P, GS * E], F32, tag="T")
            v_ps = pst.tile([P, GS * E], F32, tag="V")
            for dst, blks in ((t_ps, (0, 1, 2, 3)), (v_ps, (4, 5))):
                for s in range(SIZES[g]):
                    cs = slice(s * P, (s + 1) * P)
                    for n, blk in enumerate(blks):
                        nc.tensor.matmul_mx(
                            out=dst[:, cs],
                            lhsT=codes[:, cs].bitcast(FP8X4),
                            lhsT_scale=scales[:, cs],
                            rhs=wcodes[:, blk * E : (blk + 1) * E].bitcast(FP8X4),
                            rhs_scale=wscales[:, blk * E : (blk + 1) * E],
                            start=(n == 0),
                            stop=(n == len(blks) - 1),
                        )
            live[("ps", g, 0)] = t_ps
            live[("ps", g, 1)] = v_ps

        def bias_add(g, a):
            n = SIZES[g]
            dst = work.tile([P, GS * E], F32, tag="uv%d" % a, name="uv%d" % a)
            nc.vector.scalar_tensor_tensor(
                out=dst[:, 0 : n * E].rearrange("p (s f) -> p s f", f=E),
                in0=live[("ps", g, a)][:, 0 : n * E].rearrange("p (s f) -> p s f", f=E),
                scalar=C,
                in1=bh[:, a, :].unsqueeze(1).to_broadcast([P, n, E]),
                op0=ALU.mult,
                op1=ALU.add,
            )
            live[("uv", g, a)] = dst

        def neg_max(g, a):
            n = SIZES[g]
            nm = small.tile([P, 2 * GS], F32, tag="nm%d" % a, name="nm%d" % a)
            nc.vector.tensor_reduce(
                out=nm[:, 0 : 2 * n],
                in_=live[("uv", g, a)][:, 0 : n * E].rearrange("p (g j) -> p g j", j=HALF),
                axis=AX.X, op=ALU.max, negate=True,
            )
            live[("nm", g, a)] = nm

        def exp1(g):
            e1 = work.tile([P, GS * E], F32, tag="e1")
            s1 = small.tile([P, 2 * GS], F32, tag="s1")
            u_sb = live[("uv", g, 0)]
            nm1 = live[("nm", g, 0)]
            for h, hs in halves(0, 2 * SIZES[g]):
                nc.scalar.activation(
                    out=e1[:, hs], in_=u_sb[:, hs], func=ACTF.Exp, bias=nm1[:, h : h + 1], scale=1.0,
                    accum_out=s1[:, h : h + 1],
                )
            live[("e1", g)] = e1
            live[("s1", g)] = s1

        def recip1(g):
            n2 = 2 * SIZES[g]
            r1 = small.tile([P, 2 * GS], F32, tag="r1")
            nc.vector.reciprocal(out=r1[:, 0:n2], in_=live[("s1", g)][:, 0:n2])
            live[("r1", g)] = r1

        def add_v(g):
            w_t = work.tile([P, GS * E], F32, tag="w")
            e1 = live[("e1", g)]
            r1 = live[("r1", g)]
            vb_sb = live[("uv", g, 1)]
            for h, hs in halves(0, 2 * SIZES[g]):
                nc.vector.scalar_tensor_tensor(
                    out=w_t[:, hs], in0=e1[:, hs], scalar=r1[:, h : h + 1], in1=vb_sb[:, hs],
                    op0=ALU.mult, op1=ALU.add,
                )
            live[("w", g)] = w_t

        def exp2(g):
            e2 = work.tile([P, GS * E], F32, tag="e2")
            s2 = small.tile([P, 2 * GS], F32, tag="s2")
            w_t = live[("w", g)]
            nm2 = live[("nm", g, 1)]
            for h, hs in halves(0, 2 * SIZES[g]):
                nc.scalar.activation(
                    out=e2[:, hs], in_=w_t[:, hs], func=ACTF.Exp, bias=nm2[:, h : h + 1], scale=1.0,
                    accum_out=s2[:, h : h + 1],
                )
            live[("e2", g)] = e2
            live[("s2", g)] = s2

        def scale_sums(g):
            n2 = 2 * SIZES[g]
            s2c = small.tile([P, 2 * GS], F32, tag="s2c")
            nc.scalar.mul(out=s2c[:, 0:n2], in_=live[("s2", g)][:, 0:n2], mul=1.0 / C)
            live[("s2c", g)] = s2c

        def recip2(g):
            n2 = 2 * SIZES[g]
            r2c = small.tile([P, 2 * GS], F32, tag="r2c")
            nc.vector.reciprocal(out=r2c[:, 0:n2], in_=live[("s2c", g)][:, 0:n2])
            live[("r2c", g)] = r2c

        def scalar_halves(g):
            return 2 * SIZES[g] if g < NG - TAIL else 0

        def finish_scalar(g, lo, hi):
            if lo == 0:
                na_new = work.tile([P, GS * E], F32, tag="na")
                live[("na", g)] = na_new
            e2 = live[("e2", g)]
            r2c = live[("r2c", g)]
            na = live[("na", g)]
            for h, hs in halves(lo, min(hi, scalar_halves(g))):
                nc.scalar.activation(out=na[:, hs], in_=e2[:, hs], func=ACTF.Copy, scale=r2c[:, h : h + 1])

        def finish_vector(g):
            for h, hs in halves(scalar_halves(g), 2 * SIZES[g]):
                nc.vector.tensor_scalar(
                    out=live[("na", g)][:, hs], in0=live[("e2", g)][:, hs],
                    scalar1=live[("r2c", g)][:, h : h + 1], scalar2=None, op0=ALU.mult,
                )

        def finish_butterfly(g):
            n = SIZES[g]
            nv = live[("na", g)][:].rearrange("p (s h j) -> p s h j", h=2, j=HALF)
            o_t = work.tile([P, GS * E], F32, tag="o")
            o4 = o_t[:].rearrange("p (s j e) -> p s j e", j=HALF, e=2)
            if g < NG - TAIL:
                pieces = ((nc.gpsimd, 0, n),)
            else:
                pieces = ((nc.vector, n // 2, n), (nc.gpsimd, 0, n // 2))
            for eng, lo, hi in pieces:
                eng.tensor_tensor(
                    out=o4[:, lo:hi, :, 0], in0=nv[:, lo:hi, 0, :], in1=nv[:, lo:hi, 1, :], op=ALU.subtract
                )
                eng.tensor_tensor(
                    out=o4[:, lo:hi, :, 1], in0=nv[:, lo:hi, 0, :], in1=nv[:, lo:hi, 1, :], op=ALU.add
                )
            nc.sync.dma_start(
                out=ov[:, STARTS[g] : STARTS[g] + n, :].rearrange("p t f -> p (t f)"), in_=o_t[:, 0 : n * E]
            )

        def ok(g):
            return 0 <= g < NG

        for i in range(-3, NG + 4):
            ahead = i + 3 + LEAD
            if ok(ahead) and STARTS[ahead] % CH == 0 and STARTS[ahead] // CH >= 2:
                load(STARTS[ahead] // CH, ((0, CH),))
            if ok(i + 1):
                passes(i + 1)
            if ok(i + 3):
                transposes(i + 3)
            if ok(i - 4):
                finish_vector(i - 4)
                finish_butterfly(i - 4)
            if ok(i - 1):
                exp1(i - 1)
            if ok(i + 2):
                evacuate(i + 2)
            if ok(i):
                bias_add(i, 0)
                bias_add(i, 1)
                neg_max(i, 0)
            if ok(i - 1):
                recip1(i - 1)
            if ok(i):
                neg_max(i, 1)
            if ok(i - 3):
                recip2(i - 3)
            if ok(i - 1):
                add_v(i - 1)
            if ok(i + 2):
                quantise(i + 2)
            if i == -2:
                quantise_weights(512, 768)
            if i == -1:
                prepare_biases()
            if ok(i - 2):
                exp2(i - 2)
            if ok(i - 3):
                finish_scalar(i - 3, 0, 2)
            if ok(i - 2):
                scale_sums(i - 2)
            if ok(i - 3):
                finish_scalar(i - 3, 2, 2 * GS)
